import numpy as np
import ml_dtypes


def mxq(x, axis, fmt="e4m3"):
    dtype, down = {"e4m3": (ml_dtypes.float8_e4m3fn, 7), "e5m2": (ml_dtypes.float8_e5m2, 14)}[fmt]
    v = np.moveaxis(np.asarray(x, np.float32).astype(ml_dtypes.bfloat16).astype(np.float64), axis, -1)
    blocks = v.reshape(v.shape[:-1] + (-1, 32))
    amax = np.abs(blocks).max(-1, keepdims=True)
    byte = np.maximum(np.where(amax > 0, np.frexp(amax)[1] - 1 + 127, 0) - down, 1)
    scale = np.exp2(byte - 127.0)
    codes = (blocks / scale).astype(np.float32).astype(dtype).astype(np.float64)
    return np.moveaxis((codes * scale).reshape(v.shape), -1, axis)


WIDE = False


def mx_kscale(k):
    if not WIDE:
        return np.ones(k)
    levels = np.array([10, -10, 5, -5, 0])
    if k % 512:
        return np.exp2(np.random.permutation(np.resize(levels, k // 32))).repeat(32)
    a = np.empty((k // 512, 16))
    for p in range(k // 512):
        a[p, :8] = np.random.permutation(np.resize(levels, 8))
        for g in range(8):
            far = levels[np.abs(levels - a[p, g]) >= 10]
            a[p, g + 8] = far[np.random.randint(len(far))]
    return np.exp2(a.ravel()).repeat(32)


BF16 = ml_dtypes.bfloat16


def bf(x):
    return np.asarray(x, np.float32).astype(BF16)


def f64(x):
    return np.asarray(x).astype(np.float64)


N, H, S, R, T = 4096, 512, 4, 128, 128


def sigmoid(v):
    return 1.0 / (1.0 + np.exp(-v))


def setup_inputs():
    s, t = mx_kscale(H), mx_kscale(H)
    g = np.exp(np.random.standard_normal((S, N)))
    return {"encodings": bf(np.random.standard_normal((N, H)) * s),
            "alphas": bf(g / g.sum(axis=0, keepdims=True)),
            "W1": bf(np.random.standard_normal((S, H, H)) * 1.4 / np.sqrt(H) / s[None, :, None] * t[None, None, :]),
            "b1": bf(np.random.standard_normal((S, H)) * 0.3 * t[None, :]),
            "W2": bf(np.random.standard_normal((S, H, T)) * 2.0 / np.sqrt(H) / t[None, :, None]),
            "b2": bf(np.random.standard_normal((S, T)) * 0.5)}


def reference(encodings, alphas, W1, b1, W2, b2):
    h0 = np.maximum(f64(encodings), 0.0)
    h1 = np.maximum((mxq(h0, 1, "e4m3") @ mxq(f64(W1), 1, "e4m3")) + f64(b1)[:, None, :], 0.0)
    out = sigmoid((mxq(h1, 2, "e4m3") @ mxq(f64(W2), 1, "e4m3")) + f64(b2)[:, None, :])
    return np.sum(f64(alphas)[:, :, None] * out, axis=0)

@@ -1,0 +1,346 @@
+from contextlib import ExitStack
+
+import concourse.mybir as mybir
+from concourse.masks import make_identity
+
+F32 = mybir.dt.float32
+BF16 = mybir.dt.bfloat16
+U32 = mybir.dt.uint32
+U8 = mybir.dt.uint8
+FP8X4 = mybir.dt.float8_e4m3fn_x4
+ACT = mybir.ActivationFunctionType
+ALU = mybir.AluOpType
+
+P = 128
+PACK = 4
+N_TOK, H, S, T = 4096, 512, 4, 128
+CHUNK = 512
+BLOCKS = CHUNK // P
+N_CHUNKS = N_TOK // CHUNK
+HALF = CHUNK // 2
+FLOPS = 2 * S * N_TOK * H * (H + T)
+
+
+def tile_moe_pb_kernel(tc, encodings, alphas, W1, b1, W2, b2, out):
+    nc = tc.nc
+    with ExitStack() as ctx:
+        ctx.enter_context(tc.manual_schedule())
+        const = ctx.enter_context(tc.tile_pool(name="const", bufs=1))
+        work = ctx.enter_context(tc.tile_pool(name="work", bufs=2))
+        bank1 = ctx.enter_context(tc.psum_pool(name="bank1", bufs=PACK))
+        bank2 = ctx.enter_context(tc.psum_pool(name="bank2", bufs=1))
+        bankp = ctx.enter_context(tc.psum_pool(name="bankp", bufs=1))
+        bankx = ctx.enter_context(tc.psum_pool(name="bankx", bufs=2))
+
+        units = []
+        for c in range(N_CHUNKS):
+            for s in range(S):
+                if c == N_CHUNKS - 1 and s == S - 1:
+                    units.append((c, s, 0, HALF))
+                    units.append((c, s, HALF, HALF))
+                else:
+                    units.append((c, s, 0, CHUNK))
+        n_whole = len(units) - 2
+
+        enc_v = encodings.rearrange("(c b p) k -> c p b k", p=P, b=BLOCKS)
+        out_v = out.rearrange("(c b p) t -> c p b t", p=P, b=BLOCKS)
+        w1raw = const.tile([P, S, PACK, H], BF16)
+        w2raw = const.tile([P, S, PACK, T], BF16)
+        b1raw = const.tile([P, H], BF16)
+        b2raw = const.tile([P, P], BF16)
+        alraw = const.tile([P, P], BF16)
+        zero = const.tile([P, 1], F32)
+        warm = const.tile([P, 1], F32)
+        nc.vector.memset(b1raw[:], 0.0)
+        nc.vector.memset(b2raw[:], 0.0)
+        nc.vector.memset(zero[:], 0.0)
+        xs = []
+        for c in range(N_CHUNKS):
+            x_c = const.tile([P, BLOCKS, H], BF16, name="x%d" % c)
+            xs.append(x_c)
+
+        def load_w1(s):
+            nc.sync.dma_start(
+                out=w1raw[:, s, :, :].rearrange("p t j -> p (t j)"), in_=W1[s].rearrange("(p t) j -> p (t j)", t=PACK)
+            )
+
+        nc.scalar.dma_start(out=b1raw[0:S, :], in_=b1)
+        nc.scalar.dma_start(out=b2raw[0:S, :], in_=b2)
+        nc.scalar.dma_start(out=alraw[:], in_=alphas.rearrange("s (n p) -> (s n) p", p=P))
+        nc.sync.dma_start(out=xs[0][:, 0:2, :], in_=enc_v[0][:, 0:2, :])
+        nc.sync.dma_start(out=xs[0][:, 2:4, :], in_=enc_v[0][:, 2:4, :])
+        load_w1(0)
+        load_w1(1)
+        nc.sync.dma_start(
+            out=w2raw[:].rearrange("p s t c -> p s (t c)"), in_=W2.rearrange("s (p t) c -> p s (t c)", t=PACK)
+        )
+        load_w1(2)
+        nc.sync.dma_start(out=xs[1][:], in_=enc_v[1])
+        load_w1(3)
+        for c in range(2, N_CHUNKS):
+            nc.sync.dma_start(out=xs[c][:], in_=enc_v[c])
+
+        ident_f = const.tile([P, P], F32)
+        make_identity(nc, ident_f[:])
+        ident_b = const.tile([P, P], BF16)
+        make_identity(nc, ident_b[:])
+        nc.scalar.activation(out=warm[:], in_=zero[:], func=ACT.Sigmoid)
+
+        w1w = const.tile([P, S, H], U32, align_bytes=64)
+        w1s = const.tile([P, S, H], U8, align_bytes=64)
+        w2w = const.tile([P, S, T], U32, align_bytes=64)
+        w2s = const.tile([P, S, T], U8, align_bytes=64)
+        w2g = const.tile([P, S, T, PACK], BF16, align_bytes=64)
+        h0w = const.tile([P, N_CHUNKS, CHUNK], U32, align_bytes=64)
+        h0s = const.tile([P, N_CHUNKS, CHUNK], U8, align_bytes=64)
+        biasT = const.tile([P, PACK + 1, S], F32)
+        alT = const.tile([P, P], F32)
+
+        live = {}
+
+        def h0_transposes(c):
+            words = xs[c][:].bitcast(F32)
+            for pair in range(2):
+                turned = bankx.tile([P, 2, 2, P], F32, tag="turned", name="turned")
+                live[("turned", c, pair)] = turned
+                for b in range(2):
+                    for u in range(2):
+                        nc.tensor.transpose(
+                            turned[:, b, u, :], words[:, 2 * pair + b, u : 2 * P : 2], ident_f[:]
+                        )
+            live[("h0g", c)] = work.tile([P, CHUNK, PACK], BF16, align_bytes=64, tag="h0g", name="h0g")
+
+        def h0_copy(c, pair, on_scalar):
+            view = live[("turned", c, pair)][:].bitcast(BF16)
+            for b in range(2):
+                n0 = P * (2 * pair + b)
+                dst = live[("h0g", c)][:, n0 : n0 + P, :].rearrange("p n (u e) -> p n u e", u=2)
+                src = view[:, b, :, :].rearrange("p u (n e) -> p n u e", e=2)
+                if on_scalar:
+                    nc.scalar.activation(out=dst, in_=src, func=ACT.Relu)
+                else:
+                    nc.vector.tensor_scalar_max(out=dst, in0=src, scalar1=0.0)
+
+        def h0_quant(c, lo, n):
+            nc.vector.quantize_mx(
+                out=h0w[:, c, lo : lo + n].bitcast(FP8X4),
+                scales=h0s[:, c, lo : lo + n],
+                in_=live[("h0g", c)][:, lo : lo + n, :].rearrange("p n t -> p (n t)"),
+            )
+
+        def side_by_side(dst, src):
+            nc.vector.tensor_copy(
+                out=dst.rearrange("p (c i) t -> p c t i", i=4), in_=src.rearrange("p t (c i) -> p c t i", i=4)
+            )
+
+        def w1_regroup(s, lo, n):
+            if lo == 0:
+                live[("w1g", s)] = work.tile([P, H, PACK], BF16, align_bytes=64, tag="w1g", name="w1g")
+            src = w1raw[:, s, :, :].rearrange("p j (m t) -> p t j m", t=PACK)
+            for t in range(lo // P, (lo + n) // P):
+                side_by_side(live[("w1g", s)][:, P * t : P * t + P, :], src[:, t, :, :])
+
+        def w1_quant(s, lo, n):
+            nc.vector.quantize_mx(
+                out=w1w[:, s, lo : lo + n].bitcast(FP8X4),
+                scales=w1s[:, s, lo : lo + n],
+                in_=live[("w1g", s)][:, lo : lo + n, :].rearrange("p n t -> p (n t)"),
+            )
+
+        def w2_regroup():
+            nc.scalar.copy(out=w2g[:], in_=w2raw[:].rearrange("p s t c -> p s c t"))
+
+        def w2_quant():
+            nc.vector.quantize_mx(
+                out=w2w[:].rearrange("p s c -> p (s c)").bitcast(FP8X4),
+                scales=w2s[:].rearrange("p s c -> p (s c)"),
+                in_=w2g[:].rearrange("p s c t -> p (s c t)"),
+            )
+
+        def stage1(i, t):
+            c, s, lo, n = units[i]
+            acc1 = bank1.tile([P, CHUNK], F32, tag="acc1", name="acc1")
+            live[("acc1", i, t)] = acc1
+            nc.tensor.matmul_mx(
+                out=acc1[:, 0:n],
+                lhsT=w1w[:, s, P * t : P * t + P].bitcast(FP8X4),
+                lhsT_scale=w1s[:, s, P * t : P * t + P],
+                rhs=h0w[:, c, lo : lo + n].bitcast(FP8X4),
+                rhs_scale=h0s[:, c, lo : lo + n],
+                start=True,
+                stop=True,
+            )
+
+        def hidden(i, t):
+            s, n = units[i][1], units[i][3]
+            if t == 0:
+                live[("planes", i)] = work.tile([P, PACK, CHUNK], BF16, tag="planes", name="planes", bufs=4)
+            nc.scalar.activation(
+                out=live[("planes", i)][:, t, 0:n],
+                in_=live[("acc1", i, t)][:, 0:n],
+                func=ACT.Relu,
+                bias=biasT[:, t, s : s + 1],
+                scale=1.0,
+            )
+
+        def regroup(i):
+            n = units[i][3]
+            h1g = work.tile([P, CHUNK, PACK], BF16, align_bytes=64, tag="h1g", name="h1g", bufs=3)
+            live[("h1g", i)] = h1g
+            side_by_side(h1g[:, 0:n, :], live[("planes", i)][:, :, 0:n])
+
+        def quantise(i):
+            n = units[i][3]
+            h1w = work.tile([P, CHUNK], U32, align_bytes=64, tag="h1w", name="h1w", bufs=4)
+            h1s = work.tile([P, CHUNK], U8, align_bytes=64, tag="h1s", name="h1s", bufs=4)
+            live[("h1w", i)] = h1w
+            live[("h1s", i)] = h1s
+            nc.vector.quantize_mx(
+                out=h1w[:, 0:n].bitcast(FP8X4),
+                scales=h1s[:, 0:n],
+                in_=live[("h1g", i)][:, 0:n, :].rearrange("p n t -> p (n t)"),
+            )
+
+        def stage2(i, pool, tag):
+            s, n = units[i][1], units[i][3]
+            acc2 = pool.tile([P, CHUNK], F32, tag=tag, name="acc2")
+            live[("acc2", i)] = acc2
+            nc.tensor.matmul_mx(
+                out=acc2[:, 0:n],
+                lhsT=w2w[:, s, :].bitcast(FP8X4),
+                lhsT_scale=w2s[:, s, :],
+                rhs=live[("h1w", i)][:, 0:n].bitcast(FP8X4),
+                rhs_scale=live[("h1s", i)][:, 0:n],
+                start=True,
+                stop=True,
+            )
+
+        def sigmoid(i):
+            s, n = units[i][1], units[i][3]
+            prob = work.tile([P, CHUNK], F32, tag="prob", name="prob", bufs=4)
+            live[("prob", i)] = prob
+            nc.scalar.activation(
+                out=prob[:, 0:n], in_=live[("acc2", i)][:, 0:n], func=ACT.Sigmoid,
+                bias=biasT[:, PACK, s : s + 1], scale=1.0,
+            )
+
+        def turn_back(i, pool, tag):
+            n = units[i][3]
+            back = pool.tile([P, BLOCKS, T], F32, tag=tag, name="back")
+            live[("back", i)] = back
+            for b in range(n // P):
+                nc.tensor.transpose(back[:, b, :], live[("prob", i)][:, P * b : P * b + P], ident_f[:])
+
+        def mix(i):
+            c, s, lo, n = units[i]
+            if s == 0:
+                live[("mixed", c)] = work.tile([P, BLOCKS, T], F32, tag="mixed", name="mixed")
+            mixed = live[("mixed", c)]
+            b0 = lo // P
+            for b in range(n // P):
+                col = (N_TOK // P) * s + BLOCKS * c + b0 + b
+                if s == 0:
+                    nc.vector.tensor_scalar_mul(
+                        out=mixed[:, b0 + b, :], in0=live[("back", i)][:, b, :], scalar1=alT[:, col : col + 1]
+                    )
+                else:
+                    nc.vector.scalar_tensor_tensor(
+                        out=mixed[:, b0 + b, :],
+                        in0=live[("back", i)][:, b, :],
+                        scalar=alT[:, col : col + 1],
+                        in1=mixed[:, b0 + b, :],
+                        op0=ALU.mult,
+                        op1=ALU.add,
+                    )
+            if s == S - 1:
+                nc.sync.dma_start(out=out_v[c][:, b0 : b0 + n // P, :], in_=mixed[:, b0 : b0 + n // P, :])
+
+        h0_transposes(0)
+        smallT = bank2.tile([P, PACK + 1, P], BF16, tag="acc2", name="smallT")
+        for t in range(PACK):
+            nc.tensor.transpose(smallT[:, t, :], b1raw[:, t : H : PACK], ident_b[:])
+        nc.tensor.transpose(smallT[:, PACK, :], b2raw[:], ident_b[:])
+        alphaT = bankp.tile([P, P], BF16, tag="back", name="alphaT")
+        nc.tensor.transpose(alphaT[:], alraw[:], ident_b[:])
+        h0_copy(0, 0, False)
+        h0_copy(0, 1, True)
+        nc.vector.tensor_copy(out=biasT[:], in_=smallT[:, :, 0:S])
+        h0_quant(0, 0, HALF)
+        w1_regroup(0, 0, P)
+        h0_quant(0, HALF, HALF)
+        w1_quant(0, 0, P)
+        w1_regroup(0, P, P)
+        w1_regroup(0, 2 * P, P)
+        w1_quant(0, P, P)
+        w1_regroup(0, 3 * P, P)
+        w1_quant(0, 2 * P, P)
+        nc.vector.tensor_copy(out=alT[:], in_=alphaT[:])
+        w1_quant(0, 3 * P, P)
+        for t in range(PACK):
+            stage1(0, t)
+
+        for k in range(n_whole):
+            c, s = units[k][0], units[k][1]
+            turn_at = 2 if c == 0 else 1
+            prepare = c + 1 < N_CHUNKS
+            if k >= 3:
+                turn_back(k - 3, bankp, "back")
+            if prepare and s == turn_at:
+                h0_transposes(c + 1)
+            if k >= 2:
+                stage2(k - 2, bank2, "acc2")
+            if k + 1 < S:
+                w1_regroup(k + 1, 0, H)
+            if k >= 1:
+                regroup(k - 1)
+            if k == 1:
+                w2_regroup()
+            if prepare and s == turn_at + 1:
+                h0_quant(c + 1, 0, CHUNK)
+            if k + 1 < S:
+                w1_quant(k + 1, 0, H)
+            for t in range(PACK):
+                hidden(k, t)
+                stage1(k + 1, t)
+            if k >= 3:
+                mix(k - 3)
+            if prepare and s == turn_at:
+                h0_copy(c + 1, 0, False)
+                h0_copy(c + 1, 1, False)
+            if k >= 1:
+                quantise(k - 1)
+            if k == 1:
+                w2_quant()
+            if k >= 2:
+                sigmoid(k - 2)
+
+        a, b = n_whole, n_whole + 1
+        turn_back(a - 3, bankp, "back")
+        stage2(a - 2, bank2, "acc2")
+        regroup(a - 1)
+        for t in range(PACK):
+            hidden(a, t)
+            stage1(b, t)
+        for t in range(PACK):
+            hidden(b, t)
+        mix(a - 3)
+        quantise(a - 1)
+        sigmoid(a - 2)
+        stage2(a - 1, bank1, "acc1")
+        regroup(a)
+        regroup(b)
+        turn_back(a - 2, bankp, "back")
+        sigmoid(a - 1)
+        quantise(a)
+        stage2(a, bank1, "acc1")
+        quantise(b)
+        stage2(b, bank1, "acc1")
+        mix(a - 2)
+        turn_back(a - 1, bank1, "acc1")
+        sigmoid(a)
+        sigmoid(b)
+        mix(a - 1)
+        turn_back(a, bank2, "acc2")
+        mix(a)
+        turn_back(b, bankp, "back")
+        mix(b)

@@ -101,25 +101,23 @@ def tile_moe_pb_kernel(tc, encodings, alphas, W1, b1, W2, b2, out):
         def h0_transposes(c):
             words = xs[c][:].bitcast(F32)
             for pair in range(2):
-                turned = bankx.tile([P, 2, 2, P], F32, tag="turned", name="turned")
+                turned = bankx.tile([P, 2, 2 * P], F32, tag="turned", name="turned")
                 live[("turned", c, pair)] = turned
                 for b in range(2):
                     for u in range(2):
-                        nc.tensor.transpose(
-                            turned[:, b, u, :], words[:, 2 * pair + b, u : 2 * P : 2], ident_f[:]
+                        nc.tensor.transpose(turned[:, u, P * b : P * b + P], words[:, 2 * pair + b, u : 2 * P : 2], ident_f[:]
                         )
             live[("h0g", c)] = work.tile([P, CHUNK, PACK], BF16, align_bytes=64, tag="h0g", name="h0g")
 
         def h0_copy(c, pair, on_scalar):
             view = live[("turned", c, pair)][:].bitcast(BF16)
-            for b in range(2):
-                n0 = P * (2 * pair + b)
-                dst = live[("h0g", c)][:, n0 : n0 + P, :].rearrange("p n (u e) -> p n u e", u=2)
-                src = view[:, b, :, :].rearrange("p u (n e) -> p n u e", e=2)
-                if on_scalar:
-                    nc.scalar.activation(out=dst, in_=src, func=ACT.Relu)
-                else:
-                    nc.vector.tensor_scalar_max(out=dst, in0=src, scalar1=0.0)
+            n0 = 2 * P * pair
+            dst = live[("h0g", c)][:, n0 : n0 + 2 * P, :].rearrange("p n (u e) -> p n u e", u=2)
+            src = view.rearrange("p u (n e) -> p n u e", e=2)
+            if on_scalar:
+                nc.scalar.activation(out=dst, in_=src, func=ACT.Relu)
+            else:
+                nc.vector.tensor_scalar_max(out=dst, in0=src, scalar1=0.0)
 
         def h0_quant(c, lo, n):
             nc.vector.quantize_mx(
@@ -236,18 +234,20 @@ def tile_moe_pb_kernel(tc, encodings, alphas, W1, b1, W2, b2, out):
             if s == 0:
                 live[("mixed", c)] = work.tile([P, BLOCKS, T], F32, tag="mixed", name="mixed")
             mixed = live[("mixed", c)]
-            b0 = lo // P
-            for b in range(n // P):
-                col = (N_TOK // P) * s + BLOCKS * c + b0 + b
-                if s == 0:
-                    nc.vector.tensor_scalar_mul(
-                        out=mixed[:, b0 + b, :], in0=live[("back", i)][:, b, :], scalar1=alT[:, col : col + 1]
-                    )
-                else:
+            b0, nb = lo // P, n // P
+            col = (N_TOK // P) * s + BLOCKS * c + b0
+            if s == 0:
+                nc.vector.tensor_mul(
+                    out=mixed[:, b0 : b0 + nb, :],
+                    in0=live[("back", i)][:, 0:nb, :],
+                    in1=alT[:, col : col + nb].unsqueeze(2).broadcast_to([P, nb, T]),
+                )
+            else:
+                for b in range(nb):
                     nc.vector.scalar_tensor_tensor(
                         out=mixed[:, b0 + b, :],
                         in0=live[("back", i)][:, b, :],
-                        scalar=alT[:, col : col + 1],
+                        scalar=alT[:, col + b : col + b + 1],
                         in1=mixed[:, b0 + b, :],
                         op0=ALU.mult,
                         op1=ALU.add,

@@ -18,6 +18,8 @@ CHUNK = 512
 BLOCKS = CHUNK // P
 N_CHUNKS = N_TOK // CHUNK
 HALF = CHUNK // 2
+GPSIMD_TOKENS = 64
+STEP = 8
 FLOPS = 2 * S * N_TOK * H * (H + T)
 
 
@@ -185,7 +187,20 @@ def tile_moe_pb_kernel(tc, encodings, alphas, W1, b1, W2, b2, out):
             n = units[i][3]
             h1g = work.tile([P, CHUNK, PACK], BF16, align_bytes=64, tag="h1g", name="h1g", bufs=3)
             live[("h1g", i)] = h1g
-            side_by_side(h1g[:, 0:n, :], live[("planes", i)][:, :, 0:n])
+            planes = live[("planes", i)]
+            if n < CHUNK:
+                side_by_side(h1g[:, 0:n, :], planes[:, :, 0:n])
+            else:
+                cut = n - GPSIMD_TOKENS
+                side_by_side(h1g[:, 0 : cut + STEP, :], planes[:, :, 0 : cut + STEP])
+                nc.gpsimd.tensor_scalar(
+                    out=h1g[:, cut:n, :],
+                    in0=planes[:, :, cut:n].rearrange("p t n -> p n t"),
+                    scalar1=1.0,
+                    scalar2=0.0,
+                    op0=ALU.mult,
+                    op1=ALU.add,
+                )
 
         def quantise(i):
             n = units[i][3]

@@ -34,15 +34,30 @@ def tile_moe_pb_kernel(tc, encodings, alphas, W1, b1, W2, b2, out):
         bankp = ctx.enter_context(tc.psum_pool(name="bankp", bufs=1))
         bankx = ctx.enter_context(tc.psum_pool(name="bankx", bufs=2))
 
+        order, chunks, sources = [(0, 0)], [0], [0]
+        while len(order) < N_CHUNKS * S:
+            if len(sources) < S and len(sources) <= len(chunks):
+                s = len(sources)
+                order += [(c, s) for c in chunks]
+                sources.append(s)
+            else:
+                c = len(chunks)
+                order += [(c, s) for s in sources]
+                chunks.append(c)
         units = []
-        for c in range(N_CHUNKS):
-            for s in range(S):
-                if c == N_CHUNKS - 1 and s == S - 1:
-                    units.append((c, s, 0, HALF))
-                    units.append((c, s, HALF, HALF))
-                else:
-                    units.append((c, s, 0, CHUNK))
-        n_whole = len(units) - 2
+        for c, s in order:
+            if (c, s) == order[0]:
+                units.append((c, s, 0, HALF))
+                units.append((c, s, HALF, HALF))
+            elif (c, s) == order[-1]:
+                units.append((c, s, 0, HALF))
+                units.append((c, s, HALF, P))
+                units.append((c, s, HALF + P, P))
+            else:
+                units.append((c, s, 0, CHUNK))
+        n_whole = len(units) - 3
+        first_of_chunk = [min(i for i in range(len(units)) if units[i][0] == c) for c in range(N_CHUNKS)]
+        first_of_source = [min(i for i in range(len(units)) if units[i][1] == s) for s in range(S)]
 
         enc_v = encodings.rearrange("(c b p) k -> c p b k", p=P, b=BLOCKS)
         out_v = out.rearrange("(c b p) t -> c p b t", p=P, b=BLOCKS)
@@ -70,16 +85,17 @@ def tile_moe_pb_kernel(tc, encodings, alphas, W1, b1, W2, b2, out):
         nc.scalar.dma_start(out=b2raw[0:S, :], in_=b2)
         nc.scalar.dma_start(out=alraw[:], in_=alphas.rearrange("s (n p) -> (s n) p", p=P))
         nc.sync.dma_start(out=xs[0][:, 0:2, :], in_=enc_v[0][:, 0:2, :])
-        nc.sync.dma_start(out=xs[0][:, 2:4, :], in_=enc_v[0][:, 2:4, :])
         load_w1(0)
+        nc.sync.dma_start(out=xs[0][:, 2:4, :], in_=enc_v[0][:, 2:4, :])
         load_w1(1)
+        nc.sync.dma_start(out=xs[1][:], in_=enc_v[1])
         nc.sync.dma_start(
             out=w2raw[:].rearrange("p s t c -> p s (t c)"), in_=W2.rearrange("s (p t) c -> p s (t c)", t=PACK)
         )
         load_w1(2)
-        nc.sync.dma_start(out=xs[1][:], in_=enc_v[1])
+        nc.sync.dma_start(out=xs[2][:], in_=enc_v[2])
         load_w1(3)
-        for c in range(2, N_CHUNKS):
+        for c in range(3, N_CHUNKS):
             nc.sync.dma_start(out=xs[c][:], in_=enc_v[c])
 
         ident_f = const.tile([P, P], F32)
@@ -100,16 +116,15 @@ def tile_moe_pb_kernel(tc, encodings, alphas, W1, b1, W2, b2, out):
 
         live = {}
 
-        def h0_transposes(c):
+        def h0_transposes(c, pair):
             words = xs[c][:].bitcast(F32)
-            for pair in range(2):
-                turned = bankx.tile([P, 2, 2 * P], F32, tag="turned", name="turned")
-                live[("turned", c, pair)] = turned
-                for b in range(2):
-                    for u in range(2):
-                        nc.tensor.transpose(turned[:, u, P * b : P * b + P], words[:, 2 * pair + b, u : 2 * P : 2], ident_f[:]
-                        )
-            live[("h0g", c)] = work.tile([P, CHUNK, PACK], BF16, align_bytes=64, tag="h0g", name="h0g")
+            if pair == 0:
+                live[("h0g", c)] = work.tile([P, CHUNK, PACK], BF16, align_bytes=64, tag="h0g", name="h0g")
+            turned = bankx.tile([P, 2, 2 * P], F32, tag="turned", name="turned")
+            live[("turned", c, pair)] = turned
+            for b in range(2):
+                for u in range(2):
+                    nc.tensor.transpose(turned[:, u, P * b : P * b + P], words[:, 2 * pair + b, u : 2 * P : 2], ident_f[:])
 
         def h0_copy(c, pair, on_scalar):
             view = live[("turned", c, pair)][:].bitcast(BF16)
@@ -128,17 +143,19 @@ def tile_moe_pb_kernel(tc, encodings, alphas, W1, b1, W2, b2, out):
                 in_=live[("h0g", c)][:, lo : lo + n, :].rearrange("p n t -> p (n t)"),
             )
 
-        def side_by_side(dst, src):
-            nc.vector.tensor_copy(
-                out=dst.rearrange("p (c i) t -> p c t i", i=4), in_=src.rearrange("p t (c i) -> p c t i", i=4)
-            )
+        def side_by_side(dst, src, on_scalar=False):
+            dst = dst.rearrange("p (c i) t -> p c t i", i=4)
+            src = src.rearrange("p t (c i) -> p c t i", i=4)
+            if on_scalar:
+                nc.scalar.copy(out=dst, in_=src)
+            else:
+                nc.vector.tensor_copy(out=dst, in_=src)
 
-        def w1_regroup(s, lo, n):
-            if lo == 0:
+        def w1_regroup(s, t, on_scalar=False):
+            if ("w1g", s) not in live:
                 live[("w1g", s)] = work.tile([P, H, PACK], BF16, align_bytes=64, tag="w1g", name="w1g")
             src = w1raw[:, s, :, :].rearrange("p j (m t) -> p t j m", t=PACK)
-            for t in range(lo // P, (lo + n) // P):
-                side_by_side(live[("w1g", s)][:, P * t : P * t + P, :], src[:, t, :, :])
+            side_by_side(live[("w1g", s)][:, P * t : P * t + P, :], src[:, t, :, :], on_scalar)
 
         def w1_quant(s, lo, n):
             nc.vector.quantize_mx(
@@ -147,14 +164,14 @@ def tile_moe_pb_kernel(tc, encodings, alphas, W1, b1, W2, b2, out):
                 in_=live[("w1g", s)][:, lo : lo + n, :].rearrange("p n t -> p (n t)"),
             )
 
-        def w2_regroup():
-            nc.scalar.copy(out=w2g[:], in_=w2raw[:].rearrange("p s t c -> p s c t"))
+        def w2_regroup(s):
+            side_by_side(w2g[:, s, :, :], w2raw[:, s, :, :])
 
-        def w2_quant():
+        def w2_quant(s):
             nc.vector.quantize_mx(
-                out=w2w[:].rearrange("p s c -> p (s c)").bitcast(FP8X4),
-                scales=w2s[:].rearrange("p s c -> p (s c)"),
-                in_=w2g[:].rearrange("p s c t -> p (s c t)"),
+                out=w2w[:, s, :].bitcast(FP8X4),
+                scales=w2s[:, s, :],
+                in_=w2g[:, s, :, :].rearrange("p c t -> p (c t)"),
             )
 
         def stage1(i, t):
@@ -204,8 +221,8 @@ def tile_moe_pb_kernel(tc, encodings, alphas, W1, b1, W2, b2, out):
 
         def quantise(i):
             n = units[i][3]
-            h1w = work.tile([P, CHUNK], U32, align_bytes=64, tag="h1w", name="h1w", bufs=4)
-            h1s = work.tile([P, CHUNK], U8, align_bytes=64, tag="h1s", name="h1s", bufs=4)
+            h1w = work.tile([P, CHUNK], U32, align_bytes=64, tag="h1w", name="h1w", bufs=5)
+            h1s = work.tile([P, CHUNK], U8, align_bytes=64, tag="h1s", name="h1s", bufs=5)
             live[("h1w", i)] = h1w
             live[("h1s", i)] = h1s
             nc.vector.quantize_mx(
@@ -246,8 +263,8 @@ def tile_moe_pb_kernel(tc, encodings, alphas, W1, b1, W2, b2, out):
 
         def mix(i):
             c, s, lo, n = units[i]
-            if s == 0:
-                live[("mixed", c)] = work.tile([P, BLOCKS, T], F32, tag="mixed", name="mixed")
+            if ("mixed", c) not in live:
+                live[("mixed", c)] = work.tile([P, BLOCKS, T], F32, tag="mixed", name="mixed", bufs=4)
             mixed = live[("mixed", c)]
             b0, nb = lo // P, n // P
             col = (N_TOK // P) * s + BLOCKS * c + b0
@@ -270,7 +287,7 @@ def tile_moe_pb_kernel(tc, encodings, alphas, W1, b1, W2, b2, out):
             if s == S - 1:
                 nc.sync.dma_start(out=out_v[c][:, b0 : b0 + n // P, :], in_=mixed[:, b0 : b0 + n // P, :])
 
-        h0_transposes(0)
+        h0_transposes(0, 0)
         smallT = bank2.tile([P, PACK + 1, P], BF16, tag="acc2", name="smallT")
         for t in range(PACK):
             nc.tensor.transpose(smallT[:, t, :], b1raw[:, t : H : PACK], ident_b[:])
@@ -278,58 +295,81 @@ def tile_moe_pb_kernel(tc, encodings, alphas, W1, b1, W2, b2, out):
         alphaT = bankp.tile([P, P], BF16, tag="back", name="alphaT")
         nc.tensor.transpose(alphaT[:], alraw[:], ident_b[:])
         h0_copy(0, 0, False)
-        h0_copy(0, 1, True)
-        nc.vector.tensor_copy(out=biasT[:], in_=smallT[:, :, 0:S])
+        w1_regroup(0, 2, True)
+        w1_regroup(0, 3, True)
+        w1_regroup(0, 0)
+        nc.scalar.copy(out=biasT[:], in_=smallT[:, :, 0:S])
+        nc.scalar.copy(out=alT[:], in_=alphaT[:])
+        w1_regroup(0, 1)
         h0_quant(0, 0, HALF)
-        w1_regroup(0, 0, P)
+        w1_quant(0, 0, 2 * P)
+        h0_transposes(0, 1)
+        stage1(0, 0)
+        stage1(0, 1)
+        w1_quant(0, 2 * P, 2 * P)
+        stage1(0, 2)
+        stage1(0, 3)
+        h0_copy(0, 1, False)
         h0_quant(0, HALF, HALF)
-        w1_quant(0, 0, P)
-        w1_regroup(0, P, P)
-        w1_regroup(0, 2 * P, P)
-        w1_quant(0, P, P)
-        w1_regroup(0, 3 * P, P)
-        w1_quant(0, 2 * P, P)
-        nc.vector.tensor_copy(out=alT[:], in_=alphaT[:])
-        w1_quant(0, 3 * P, P)
-        for t in range(PACK):
-            stage1(0, t)
+        w1_regroup(1, 0)
+        w1_regroup(1, 1)
+        w1_regroup(1, 2)
+        w1_regroup(1, 3)
+        w1_quant(1, 0, H)
+
+        def settled(k):
+            return max(k - 2 if k <= n_whole - 4 else k - 1, 0)
 
         for k in range(n_whole):
-            c, s = units[k][0], units[k][1]
-            turn_at = 2 if c == 0 else 1
-            prepare = c + 1 < N_CHUNKS
-            if k >= 3:
-                turn_back(k - 3, bankp, "back")
-            if prepare and s == turn_at:
-                h0_transposes(c + 1)
-            if k >= 2:
-                stage2(k - 2, bank2, "acc2")
-            if k + 1 < S:
-                w1_regroup(k + 1, 0, H)
+            chunk_at = lambda j: [c for c in range(1, N_CHUNKS) if first_of_chunk[c] == j]
+            source_at = lambda j: [s for s in range(1, S) if first_of_source[s] == j]
+            early, late = chunk_at(k + 3), chunk_at(k + 2)
+            for i in range(settled(k - 2), settled(k - 1)):
+                if i == settled(k - 2):
+                    turn_back(i, bankp, "back")
+                else:
+                    turn_back(i, bankx, "turned")
+            for c in early:
+                h0_transposes(c, 0)
+                h0_transposes(c, 1)
+            for i in range(settled(k - 1), min(settled(k - 1) + 1, settled(k))):
+                stage2(i, bank2, "acc2")
+            if k > 0:
+                for s in source_at(k + 2):
+                    for t in range(PACK):
+                        w1_regroup(s, t)
             if k >= 1:
                 regroup(k - 1)
-            if k == 1:
-                w2_regroup()
-            if prepare and s == turn_at + 1:
-                h0_quant(c + 1, 0, CHUNK)
-            if k + 1 < S:
-                w1_quant(k + 1, 0, H)
+            for c in chunk_at(k + 1):
+                h0_quant(c, 0, CHUNK)
+            if k > 1:
+                for s in source_at(k + 1):
+                    w1_quant(s, 0, H)
             for t in range(PACK):
                 hidden(k, t)
                 stage1(k + 1, t)
-            if k >= 3:
-                mix(k - 3)
-            if prepare and s == turn_at:
-                h0_copy(c + 1, 0, False)
-                h0_copy(c + 1, 1, False)
-            if k >= 1:
-                quantise(k - 1)
             if k == 1:
-                w2_quant()
-            if k >= 2:
-                sigmoid(k - 2)
+                w2_regroup(0)
+            for s in source_at(k - 1):
+                w2_regroup(s)
+            for i in range(settled(k - 1) + 1, settled(k)):
+                stage2(i, bankx, "turned")
+            for i in range(settled(k - 2), settled(k - 1)):
+                mix(i)
+            for c in early:
+                h0_copy(c, 0, False)
+            for c in late:
+                h0_copy(c, 1, False)
+            for i in range(settled(k), settled(k + 1)):
+                quantise(i)
+            if k == 1:
+                w2_quant(0)
+            for s in source_at(k - 1):
+                w2_quant(s)
+            for i in range(settled(k - 1), settled(k)):
+                sigmoid(i)
 
-        a, b = n_whole, n_whole + 1
+        a, b, d = n_whole, n_whole + 1, n_whole + 2
         turn_back(a - 3, bankp, "back")
         stage2(a - 2, bank2, "acc2")
         regroup(a - 1)
@@ -338,24 +378,33 @@ def tile_moe_pb_kernel(tc, encodings, alphas, W1, b1, W2, b2, out):
             stage1(b, t)
         for t in range(PACK):
             hidden(b, t)
+            stage1(d, t)
+        for t in range(PACK):
+            hidden(d, t)
         mix(a - 3)
         quantise(a - 1)
         sigmoid(a - 2)
-        stage2(a - 1, bank1, "acc1")
         regroup(a)
+        stage2(a - 1, bank1, "acc1")
         regroup(b)
-        turn_back(a - 2, bankp, "back")
-        sigmoid(a - 1)
         quantise(a)
-        stage2(a, bank1, "acc1")
+        regroup(d)
         quantise(b)
+        sigmoid(a - 1)
+        turn_back(a - 2, bankp, "back")
+        quantise(d)
+        stage2(a, bank1, "acc1")
         stage2(b, bank1, "acc1")
+        stage2(d, bank1, "acc1")
         mix(a - 2)
-        turn_back(a - 1, bank1, "acc1")
+        turn_back(a - 1, bank2, "acc2")
+        mix(a - 1)
         sigmoid(a)
         sigmoid(b)
-        mix(a - 1)
-        turn_back(a, bank2, "acc2")
+        sigmoid(d)
+        turn_back(a, bankp, "back")
         mix(a)
-        turn_back(b, bankp, "back")
+        turn_back(b, bankx, "turned")
         mix(b)
+        turn_back(d, bankx, "turned")
+        mix(d)

@@ -63,12 +63,11 @@ def tile_moe_pb_kernel(tc, encodings, alphas, W1, b1, W2, b2, out):
         out_v = out.rearrange("(c b p) t -> c p b t", p=P, b=BLOCKS)
         w1raw = const.tile([P, S, PACK, H], BF16)
         w2raw = const.tile([P, S, PACK, T], BF16)
-        b1raw = const.tile([P, H], BF16)
+        b1T = const.tile([P, S, PACK], BF16)
         b2raw = const.tile([P, P], BF16)
         alraw = const.tile([P, P], BF16)
         zero = const.tile([P, 1], F32)
         warm = const.tile([P, 1], F32)
-        nc.vector.memset(b1raw[:], 0.0)
         nc.vector.memset(b2raw[:], 0.0)
         nc.vector.memset(zero[:], 0.0)
         xs = []
@@ -81,7 +80,7 @@ def tile_moe_pb_kernel(tc, encodings, alphas, W1, b1, W2, b2, out):
                 out=w1raw[:, s, :, :].rearrange("p t j -> p (t j)"), in_=W1[s].rearrange("(p t) j -> p (t j)", t=PACK)
             )
 
-        nc.scalar.dma_start(out=b1raw[0:S, :], in_=b1)
+        nc.scalar.dma_start(out=b1T[:], in_=b1.rearrange("s (p t) -> p s t", t=PACK))
         nc.scalar.dma_start(out=b2raw[0:S, :], in_=b2)
         nc.scalar.dma_start(out=alraw[:], in_=alphas.rearrange("s (n p) -> (s n) p", p=P))
         nc.sync.dma_start(out=xs[0][:, 0:2, :], in_=enc_v[0][:, 0:2, :])
@@ -111,7 +110,7 @@ def tile_moe_pb_kernel(tc, encodings, alphas, W1, b1, W2, b2, out):
         w2g = const.tile([P, S, T, PACK], BF16, align_bytes=64)
         h0w = const.tile([P, N_CHUNKS, CHUNK], U32, align_bytes=64)
         h0s = const.tile([P, N_CHUNKS, CHUNK], U8, align_bytes=64)
-        biasT = const.tile([P, PACK + 1, S], F32)
+        b2T = const.tile([P, S], F32)
         alT = const.tile([P, P], F32)
 
         live = {}
@@ -196,7 +195,7 @@ def tile_moe_pb_kernel(tc, encodings, alphas, W1, b1, W2, b2, out):
                 out=live[("planes", i)][:, t, 0:n],
                 in_=live[("acc1", i, t)][:, 0:n],
                 func=ACT.Relu,
-                bias=biasT[:, t, s : s + 1],
+                bias=b1T[:, s, t : t + 1],
                 scale=1.0,
             )
 
@@ -251,7 +250,7 @@ def tile_moe_pb_kernel(tc, encodings, alphas, W1, b1, W2, b2, out):
             live[("prob", i)] = prob
             nc.scalar.activation(
                 out=prob[:, 0:n], in_=live[("acc2", i)][:, 0:n], func=ACT.Sigmoid,
-                bias=biasT[:, PACK, s : s + 1], scale=1.0,
+                bias=b2T[:, s : s + 1], scale=1.0,
             )
 
         def turn_back(i, pool, tag):
@@ -288,18 +287,10 @@ def tile_moe_pb_kernel(tc, encodings, alphas, W1, b1, W2, b2, out):
                 nc.sync.dma_start(out=out_v[c][:, b0 : b0 + n // P, :], in_=mixed[:, b0 : b0 + n // P, :])
 
         h0_transposes(0, 0)
-        smallT = bank2.tile([P, PACK + 1, P], BF16, tag="acc2", name="smallT")
-        for t in range(PACK):
-            nc.tensor.transpose(smallT[:, t, :], b1raw[:, t : H : PACK], ident_b[:])
-        nc.tensor.transpose(smallT[:, PACK, :], b2raw[:], ident_b[:])
-        alphaT = bankp.tile([P, P], BF16, tag="back", name="alphaT")
-        nc.tensor.transpose(alphaT[:], alraw[:], ident_b[:])
         h0_copy(0, 0, False)
         w1_regroup(0, 2, True)
         w1_regroup(0, 3, True)
         w1_regroup(0, 0)
-        nc.scalar.copy(out=biasT[:], in_=smallT[:, :, 0:S])
-        nc.scalar.copy(out=alT[:], in_=alphaT[:])
         w1_regroup(0, 1)
         h0_quant(0, 0, HALF)
         w1_quant(0, 0, 2 * P)
@@ -329,6 +320,11 @@ def tile_moe_pb_kernel(tc, encodings, alphas, W1, b1, W2, b2, out):
                     turn_back(i, bankp, "back")
                 else:
                     turn_back(i, bankx, "turned")
+            if k == 1:
+                b2turned = bank2.tile([P, P], BF16, tag="acc2", name="b2turned")
+                nc.tensor.transpose(b2turned[:], b2raw[:], ident_b[:])
+                alphaT = bankp.tile([P, P], BF16, tag="back", name="alphaT")
+                nc.tensor.transpose(alphaT[:], alraw[:], ident_b[:])
             for c in early:
                 h0_transposes(c, 0)
                 h0_transposes(c, 1)
@@ -349,6 +345,8 @@ def tile_moe_pb_kernel(tc, encodings, alphas, W1, b1, W2, b2, out):
                 hidden(k, t)
                 stage1(k + 1, t)
             if k == 1:
+                nc.scalar.copy(out=b2T[:], in_=b2turned[:, 0:S])
+                nc.scalar.copy(out=alT[:], in_=alphaT[:])
                 w2_regroup(0)
             for s in source_at(k - 1):
                 w2_regroup(s)

@@ -18,7 +18,7 @@ CHUNK = 512
 BLOCKS = CHUNK // P
 N_CHUNKS = N_TOK // CHUNK
 HALF = CHUNK // 2
-GPSIMD_TOKENS = 64
+GPSIMD_TOKENS = 96
 STEP = 8
 FLOPS = 2 * S * N_TOK * H * (H + T)
 
@@ -188,16 +188,14 @@ def tile_moe_pb_kernel(tc, encodings, alphas, W1, b1, W2, b2, out):
             )
 
         def hidden(i, t):
-            s, n = units[i][1], units[i][3]
+            c, s, lo, n = units[i]
             if t == 0:
                 live[("planes", i)] = work.tile([P, PACK, CHUNK], BF16, tag="planes", name="planes", bufs=4)
-            nc.scalar.activation(
-                out=live[("planes", i)][:, t, 0:n],
-                in_=live[("acc1", i, t)][:, 0:n],
-                func=ACT.Relu,
-                bias=b1T[:, s, t : t + 1],
-                scale=1.0,
-            )
+            out, acc, bias = live[("planes", i)][:, t, 0:n], live[("acc1", i, t)][:, 0:n], b1T[:, s, t : t + 1]
+            if t == PACK - 1 and (s == 0 and c >= N_CHUNKS // 2):
+                nc.vector.tensor_scalar(out=out, in0=acc, scalar1=bias, scalar2=0.0, op0=ALU.add, op1=ALU.max)
+            else:
+                nc.scalar.activation(out=out, in_=acc, func=ACT.Relu, bias=bias, scale=1.0)
 
         def regroup(i):
             n = units[i][3]
@@ -300,11 +298,11 @@ def tile_moe_pb_kernel(tc, encodings, alphas, W1, b1, W2, b2, out):
         w1_quant(0, 2 * P, 2 * P)
         stage1(0, 2)
         stage1(0, 3)
-        h0_copy(0, 1, False)
-        h0_quant(0, HALF, HALF)
+        h0_copy(0, 1, True)
         w1_regroup(1, 0)
         w1_regroup(1, 1)
         w1_regroup(1, 2)
+        h0_quant(0, HALF, HALF)
         w1_regroup(1, 3)
         w1_quant(1, 0, H)
 
@@ -355,7 +353,7 @@ def tile_moe_pb_kernel(tc, encodings, alphas, W1, b1, W2, b2, out):
             for i in range(settled(k - 2), settled(k - 1)):
                 mix(i)
             for c in early:
-                h0_copy(c, 0, False)
+                h0_copy(c, 0, c == 1)
             for c in late:
                 h0_copy(c, 1, False)
             for i in range(settled(k), settled(k + 1)):

@@ -18,7 +18,8 @@ CHUNK = 512
 BLOCKS = CHUNK // P
 N_CHUNKS = N_TOK // CHUNK
 HALF = CHUNK // 2
-GPSIMD_TOKENS = 96
+SHARE, LONG_SHARE = 96, 160
+FULL_FROM = 3
 STEP = 8
 FLOPS = 2 * S * N_TOK * H * (H + T)
 
@@ -187,25 +188,29 @@ def tile_moe_pb_kernel(tc, encodings, alphas, W1, b1, W2, b2, out):
                 stop=True,
             )
 
-        def hidden(i, t):
+        def vector_empties(i):
             c, s, lo, n = units[i]
+            return s == 0 and c >= FULL_FROM
+
+        def hidden(i, t):
+            s, n = units[i][1], units[i][3]
             if t == 0:
                 live[("planes", i)] = work.tile([P, PACK, CHUNK], BF16, tag="planes", name="planes", bufs=4)
             out, acc, bias = live[("planes", i)][:, t, 0:n], live[("acc1", i, t)][:, 0:n], b1T[:, s, t : t + 1]
-            if t == PACK - 1 and (s == 0 and c >= N_CHUNKS // 2):
+            if t == PACK - 1 and vector_empties(i):
                 nc.vector.tensor_scalar(out=out, in0=acc, scalar1=bias, scalar2=0.0, op0=ALU.add, op1=ALU.max)
             else:
                 nc.scalar.activation(out=out, in_=acc, func=ACT.Relu, bias=bias, scale=1.0)
 
-        def regroup(i):
+        def regroup(i, share=0):
             n = units[i][3]
             h1g = work.tile([P, CHUNK, PACK], BF16, align_bytes=64, tag="h1g", name="h1g", bufs=3)
             live[("h1g", i)] = h1g
             planes = live[("planes", i)]
-            if n < CHUNK:
+            if share == 0:
                 side_by_side(h1g[:, 0:n, :], planes[:, :, 0:n])
             else:
-                cut = n - GPSIMD_TOKENS
+                cut = n - share
                 side_by_side(h1g[:, 0 : cut + STEP, :], planes[:, :, 0 : cut + STEP])
                 nc.gpsimd.tensor_scalar(
                     out=h1g[:, cut:n, :],
@@ -307,7 +312,7 @@ def tile_moe_pb_kernel(tc, encodings, alphas, W1, b1, W2, b2, out):
         w1_quant(1, 0, H)
 
         def settled(k):
-            return max(k - 2 if k <= n_whole - 4 else k - 1, 0)
+            return max(k - 2 if k <= n_whole - 3 else k - 1, 0)
 
         for k in range(n_whole):
             chunk_at = lambda j: [c for c in range(1, N_CHUNKS) if first_of_chunk[c] == j]
@@ -332,7 +337,9 @@ def tile_moe_pb_kernel(tc, encodings, alphas, W1, b1, W2, b2, out):
                 for s in source_at(k + 2):
                     for t in range(PACK):
                         w1_regroup(s, t)
-            if k >= 1:
+            if k >= 1 and units[k - 1][3] == CHUNK:
+                regroup(k - 1, LONG_SHARE if early or late or vector_empties(k) else SHARE)
+            elif k >= 1:
                 regroup(k - 1)
             for c in chunk_at(k + 1):
                 h0_quant(c, 0, CHUNK)
@@ -368,7 +375,7 @@ def tile_moe_pb_kernel(tc, encodings, alphas, W1, b1, W2, b2, out):
         a, b, d = n_whole, n_whole + 1, n_whole + 2
         turn_back(a - 3, bankp, "back")
         stage2(a - 2, bank2, "acc2")
-        regroup(a - 1)
+        regroup(a - 1, SHARE)
         for t in range(PACK):
             hidden(a, t)
             stage1(b, t)

from contextlib import ExitStack

import concourse.mybir as mybir
from concourse.masks import make_identity

F32 = mybir.dt.float32
BF16 = mybir.dt.bfloat16
U32 = mybir.dt.uint32
U8 = mybir.dt.uint8
FP8X4 = mybir.dt.float8_e4m3fn_x4
ACT = mybir.ActivationFunctionType
ALU = mybir.AluOpType

P = 128
PACK = 4
N_TOK, H, S, T = 4096, 512, 4, 128
CHUNK = 512
BLOCKS = CHUNK // P
N_CHUNKS = N_TOK // CHUNK
HALF = CHUNK // 2
SHARE, LONG_SHARE = 96, 160
FULL_FROM = 3
STEP = 8
FLOPS = 2 * S * N_TOK * H * (H + T)


def tile_moe_pb_kernel(tc, encodings, alphas, W1, b1, W2, b2, out):
    nc = tc.nc
    with ExitStack() as ctx:
        ctx.enter_context(tc.manual_schedule())
        const = ctx.enter_context(tc.tile_pool(name="const", bufs=1))
        work = ctx.enter_context(tc.tile_pool(name="work", bufs=2))
        bank1 = ctx.enter_context(tc.psum_pool(name="bank1", bufs=PACK))
        bank2 = ctx.enter_context(tc.psum_pool(name="bank2", bufs=1))
        bankp = ctx.enter_context(tc.psum_pool(name="bankp", bufs=1))
        bankx = ctx.enter_context(tc.psum_pool(name="bankx", bufs=2))

        order, chunks, sources = [(0, 0)], [0], [0]
        while len(order) < N_CHUNKS * S:
            if len(sources) < S and len(sources) <= len(chunks):
                s = len(sources)
                order += [(c, s) for c in chunks]
                sources.append(s)
            else:
                c = len(chunks)
                order += [(c, s) for s in sources]
                chunks.append(c)
        units = []
        for c, s in order:
            if (c, s) == order[0]:
                units.append((c, s, 0, HALF))
                units.append((c, s, HALF, HALF))
            elif (c, s) == order[-1]:
                units.append((c, s, 0, HALF))
                units.append((c, s, HALF, P))
                units.append((c, s, HALF + P, P))
            else:
                units.append((c, s, 0, CHUNK))
        n_whole = len(units) - 3
        first_of_chunk = [min(i for i in range(len(units)) if units[i][0] == c) for c in range(N_CHUNKS)]
        first_of_source = [min(i for i in range(len(units)) if units[i][1] == s) for s in range(S)]

        enc_v = encodings.rearrange("(c b p) k -> c p b k", p=P, b=BLOCKS)
        out_v = out.rearrange("(c b p) t -> c p b t", p=P, b=BLOCKS)
        w1raw = const.tile([P, S, PACK, H], BF16)
        w2raw = const.tile([P, S, PACK, T], BF16)
        b1T = const.tile([P, S, PACK], BF16)
        b2raw = const.tile([P, P], BF16)
        alraw = const.tile([P, P], BF16)
        zero = const.tile([P, 1], F32)
        warm = const.tile([P, 1], F32)
        nc.vector.memset(b2raw[:], 0.0)
        nc.vector.memset(zero[:], 0.0)
        xs = []
        for c in range(N_CHUNKS):
            x_c = const.tile([P, BLOCKS, H], BF16, name="x%d" % c)
            xs.append(x_c)

        def load_w1(s):
            nc.sync.dma_start(
                out=w1raw[:, s, :, :].rearrange("p t j -> p (t j)"), in_=W1[s].rearrange("(p t) j -> p (t j)", t=PACK)
            )

        nc.scalar.dma_start(out=b1T[:], in_=b1.rearrange("s (p t) -> p s t", t=PACK))
        nc.scalar.dma_start(out=b2raw[0:S, :], in_=b2)
        nc.scalar.dma_start(out=alraw[:], in_=alphas.rearrange("s (n p) -> (s n) p", p=P))
        nc.sync.dma_start(out=xs[0][:, 0:2, :], in_=enc_v[0][:, 0:2, :])
        load_w1(0)
        nc.sync.dma_start(out=xs[0][:, 2:4, :], in_=enc_v[0][:, 2:4, :])
        load_w1(1)
        nc.sync.dma_start(out=xs[1][:], in_=enc_v[1])
        nc.sync.dma_start(
            out=w2raw[:].rearrange("p s t c -> p s (t c)"), in_=W2.rearrange("s (p t) c -> p s (t c)", t=PACK)
        )
        load_w1(2)
        nc.sync.dma_start(out=xs[2][:], in_=enc_v[2])
        load_w1(3)
        for c in range(3, N_CHUNKS):
            nc.sync.dma_start(out=xs[c][:], in_=enc_v[c])

        ident_f = const.tile([P, P], F32)
        make_identity(nc, ident_f[:])
        ident_b = const.tile([P, P], BF16)
        make_identity(nc, ident_b[:])
        nc.scalar.activation(out=warm[:], in_=zero[:], func=ACT.Sigmoid)

        w1w = const.tile([P, S, H], U32, align_bytes=64)
        w1s = const.tile([P, S, H], U8, align_bytes=64)
        w2w = const.tile([P, S, T], U32, align_bytes=64)
        w2s = const.tile([P, S, T], U8, align_bytes=64)
        w2g = const.tile([P, S, T, PACK], BF16, align_bytes=64)
        h0w = const.tile([P, N_CHUNKS, CHUNK], U32, align_bytes=64)
        h0s = const.tile([P, N_CHUNKS, CHUNK], U8, align_bytes=64)
        b2T = const.tile([P, S], F32)
        alT = const.tile([P, P], F32)

        live = {}

        def h0_transposes(c, pair):
            words = xs[c][:].bitcast(F32)
            if pair == 0:
                live[("h0g", c)] = work.tile([P, CHUNK, PACK], BF16, align_bytes=64, tag="h0g", name="h0g")
            turned = bankx.tile([P, 2, 2 * P], F32, tag="turned", name="turned")
            live[("turned", c, pair)] = turned
            for b in range(2):
                for u in range(2):
                    nc.tensor.transpose(turned[:, u, P * b : P * b + P], words[:, 2 * pair + b, u : 2 * P : 2], ident_f[:])

        def h0_copy(c, pair, on_scalar):
            view = live[("turned", c, pair)][:].bitcast(BF16)
            n0 = 2 * P * pair
            dst = live[("h0g", c)][:, n0 : n0 + 2 * P, :].rearrange("p n (u e) -> p n u e", u=2)
            src = view.rearrange("p u (n e) -> p n u e", e=2)
            if on_scalar:
                nc.scalar.activation(out=dst, in_=src, func=ACT.Relu)
            else:
                nc.vector.tensor_scalar_max(out=dst, in0=src, scalar1=0.0)

        def h0_quant(c, lo, n):
            nc.vector.quantize_mx(
                out=h0w[:, c, lo : lo + n].bitcast(FP8X4),
                scales=h0s[:, c, lo : lo + n],
                in_=live[("h0g", c)][:, lo : lo + n, :].rearrange("p n t -> p (n t)"),
            )

        def side_by_side(dst, src, on_scalar=False):
            dst = dst.rearrange("p (c i) t -> p c t i", i=4)
            src = src.rearrange("p t (c i) -> p c t i", i=4)
            if on_scalar:
                nc.scalar.copy(out=dst, in_=src)
            else:
                nc.vector.tensor_copy(out=dst, in_=src)

        def w1_regroup(s, t, on_scalar=False):
            if ("w1g", s) not in live:
                live[("w1g", s)] = work.tile([P, H, PACK], BF16, align_bytes=64, tag="w1g", name="w1g")
            src = w1raw[:, s, :, :].rearrange("p j (m t) -> p t j m", t=PACK)
            side_by_side(live[("w1g", s)][:, P * t : P * t + P, :], src[:, t, :, :], on_scalar)

        def w1_quant(s, lo, n):
            nc.vector.quantize_mx(
                out=w1w[:, s, lo : lo + n].bitcast(FP8X4),
                scales=w1s[:, s, lo : lo + n],
                in_=live[("w1g", s)][:, lo : lo + n, :].rearrange("p n t -> p (n t)"),
            )

        def w2_regroup(s):
            side_by_side(w2g[:, s, :, :], w2raw[:, s, :, :])

        def w2_quant(s):
            nc.vector.quantize_mx(
                out=w2w[:, s, :].bitcast(FP8X4),
                scales=w2s[:, s, :],
                in_=w2g[:, s, :, :].rearrange("p c t -> p (c t)"),
            )

        def stage1(i, t):
            c, s, lo, n = units[i]
            acc1 = bank1.tile([P, CHUNK], F32, tag="acc1", name="acc1")
            live[("acc1", i, t)] = acc1
            nc.tensor.matmul_mx(
                out=acc1[:, 0:n],
                lhsT=w1w[:, s, P * t : P * t + P].bitcast(FP8X4),
                lhsT_scale=w1s[:, s, P * t : P * t + P],
                rhs=h0w[:, c, lo : lo + n].bitcast(FP8X4),
                rhs_scale=h0s[:, c, lo : lo + n],
                start=True,
                stop=True,
            )

        def vector_empties(i):
            c, s, lo, n = units[i]
            return s == 0 and c >= FULL_FROM

        def hidden(i, t):
            s, n = units[i][1], units[i][3]
            if t == 0:
                live[("planes", i)] = work.tile([P, PACK, CHUNK], BF16, tag="planes", name="planes", bufs=4)
            out, acc, bias = live[("planes", i)][:, t, 0:n], live[("acc1", i, t)][:, 0:n], b1T[:, s, t : t + 1]
            if t == PACK - 1 and vector_empties(i):
                nc.vector.tensor_scalar(out=out, in0=acc, scalar1=bias, scalar2=0.0, op0=ALU.add, op1=ALU.max)
            else:
                nc.scalar.activation(out=out, in_=acc, func=ACT.Relu, bias=bias, scale=1.0)

        def regroup(i, share=0):
            n = units[i][3]
            h1g = work.tile([P, CHUNK, PACK], BF16, align_bytes=64, tag="h1g", name="h1g", bufs=3)
            live[("h1g", i)] = h1g
            planes = live[("planes", i)]
            if share == 0:
                side_by_side(h1g[:, 0:n, :], planes[:, :, 0:n])
            else:
                cut = n - share
                side_by_side(h1g[:, 0 : cut + STEP, :], planes[:, :, 0 : cut + STEP])
                nc.gpsimd.tensor_scalar(
                    out=h1g[:, cut:n, :],
                    in0=planes[:, :, cut:n].rearrange("p t n -> p n t"),
                    scalar1=1.0,
                    scalar2=0.0,
                    op0=ALU.mult,
                    op1=ALU.add,
                )

        def quantise(i):
            n = units[i][3]
            h1w = work.tile([P, CHUNK], U32, align_bytes=64, tag="h1w", name="h1w", bufs=5)
            h1s = work.tile([P, CHUNK], U8, align_bytes=64, tag="h1s", name="h1s", bufs=5)
            live[("h1w", i)] = h1w
            live[("h1s", i)] = h1s
            nc.vector.quantize_mx(
                out=h1w[:, 0:n].bitcast(FP8X4),
                scales=h1s[:, 0:n],
                in_=live[("h1g", i)][:, 0:n, :].rearrange("p n t -> p (n t)"),
            )

        def stage2(i, pool, tag):
            s, n = units[i][1], units[i][3]
            acc2 = pool.tile([P, CHUNK], F32, tag=tag, name="acc2")
            live[("acc2", i)] = acc2
            nc.tensor.matmul_mx(
                out=acc2[:, 0:n],
                lhsT=w2w[:, s, :].bitcast(FP8X4),
                lhsT_scale=w2s[:, s, :],
                rhs=live[("h1w", i)][:, 0:n].bitcast(FP8X4),
                rhs_scale=live[("h1s", i)][:, 0:n],
                start=True,
                stop=True,
            )

        def sigmoid(i):
            s, n = units[i][1], units[i][3]
            prob = work.tile([P, CHUNK], F32, tag="prob", name="prob", bufs=4)
            live[("prob", i)] = prob
            nc.scalar.activation(
                out=prob[:, 0:n], in_=live[("acc2", i)][:, 0:n], func=ACT.Sigmoid,
                bias=b2T[:, s : s + 1], scale=1.0,
            )

        def turn_back(i, pool, tag):
            n = units[i][3]
            back = pool.tile([P, BLOCKS, T], F32, tag=tag, name="back")
            live[("back", i)] = back
            for b in range(n // P):
                nc.tensor.transpose(back[:, b, :], live[("prob", i)][:, P * b : P * b + P], ident_f[:])

        def mix(i):
            c, s, lo, n = units[i]
            if ("mixed", c) not in live:
                live[("mixed", c)] = work.tile([P, BLOCKS, T], F32, tag="mixed", name="mixed", bufs=4)
            mixed = live[("mixed", c)]
            b0, nb = lo // P, n // P
            col = (N_TOK // P) * s + BLOCKS * c + b0
            if s == 0:
                nc.vector.tensor_mul(
                    out=mixed[:, b0 : b0 + nb, :],
                    in0=live[("back", i)][:, 0:nb, :],
                    in1=alT[:, col : col + nb].unsqueeze(2).broadcast_to([P, nb, T]),
                )
            else:
                for b in range(nb):
                    nc.vector.scalar_tensor_tensor(
                        out=mixed[:, b0 + b, :],
                        in0=live[("back", i)][:, b, :],
                        scalar=alT[:, col + b : col + b + 1],
                        in1=mixed[:, b0 + b, :],
                        op0=ALU.mult,
                        op1=ALU.add,
                    )
            if s == S - 1:
                nc.sync.dma_start(out=out_v[c][:, b0 : b0 + n // P, :], in_=mixed[:, b0 : b0 + n // P, :])

        h0_transposes(0, 0)
        h0_copy(0, 0, False)
        w1_regroup(0, 2, True)
        w1_regroup(0, 3, True)
        w1_regroup(0, 0)
        w1_regroup(0, 1)
        h0_quant(0, 0, HALF)
        w1_quant(0, 0, 2 * P)
        h0_transposes(0, 1)
        stage1(0, 0)
        stage1(0, 1)
        w1_quant(0, 2 * P, 2 * P)
        stage1(0, 2)
        stage1(0, 3)
        h0_copy(0, 1, True)
        w1_regroup(1, 0)
        w1_regroup(1, 1)
        w1_regroup(1, 2)
        h0_quant(0, HALF, HALF)
        w1_regroup(1, 3)
        w1_quant(1, 0, H)

        def settled(k):
            return max(k - 2 if k <= n_whole - 3 else k - 1, 0)

        for k in range(n_whole):
            chunk_at = lambda j: [c for c in range(1, N_CHUNKS) if first_of_chunk[c] == j]
            source_at = lambda j: [s for s in range(1, S) if first_of_source[s] == j]
            early, late = chunk_at(k + 3), chunk_at(k + 2)
            for i in range(settled(k - 2), settled(k - 1)):
                if i == settled(k - 2):
                    turn_back(i, bankp, "back")
                else:
                    turn_back(i, bankx, "turned")
            if k == 1:
                b2turned = bank2.tile([P, P], BF16, tag="acc2", name="b2turned")
                nc.tensor.transpose(b2turned[:], b2raw[:], ident_b[:])
                alphaT = bankp.tile([P, P], BF16, tag="back", name="alphaT")
                nc.tensor.transpose(alphaT[:], alraw[:], ident_b[:])
            for c in early:
                h0_transposes(c, 0)
                h0_transposes(c, 1)
            for i in range(settled(k - 1), min(settled(k - 1) + 1, settled(k))):
                stage2(i, bank2, "acc2")
            if k > 0:
                for s in source_at(k + 2):
                    for t in range(PACK):
                        w1_regroup(s, t)
            if k >= 1 and units[k - 1][3] == CHUNK:
                regroup(k - 1, LONG_SHARE if early or late or vector_empties(k) else SHARE)
            elif k >= 1:
                regroup(k - 1)
            for c in chunk_at(k + 1):
                h0_quant(c, 0, CHUNK)
            if k > 1:
                for s in source_at(k + 1):
                    w1_quant(s, 0, H)
            for t in range(PACK):
                hidden(k, t)
                stage1(k + 1, t)
            if k == 1:
                nc.scalar.copy(out=b2T[:], in_=b2turned[:, 0:S])
                nc.scalar.copy(out=alT[:], in_=alphaT[:])
                w2_regroup(0)
            for s in source_at(k - 1):
                w2_regroup(s)
            for i in range(settled(k - 1) + 1, settled(k)):
                stage2(i, bankx, "turned")
            for i in range(settled(k - 2), settled(k - 1)):
                mix(i)
            for c in early:
                h0_copy(c, 0, c == 1)
            for c in late:
                h0_copy(c, 1, False)
            for i in range(settled(k), settled(k + 1)):
                quantise(i)
            if k == 1:
                w2_quant(0)
            for s in source_at(k - 1):
                w2_quant(s)
            for i in range(settled(k - 1), settled(k)):
                sigmoid(i)

        a, b, d = n_whole, n_whole + 1, n_whole + 2
        turn_back(a - 3, bankp, "back")
        stage2(a - 2, bank2, "acc2")
        regroup(a - 1, SHARE)
        for t in range(PACK):
            hidden(a, t)
            stage1(b, t)
        for t in range(PACK):
            hidden(b, t)
            stage1(d, t)
        for t in range(PACK):
            hidden(d, t)
        mix(a - 3)
        quantise(a - 1)
        sigmoid(a - 2)
        regroup(a)
        stage2(a - 1, bank1, "acc1")
        regroup(b)
        quantise(a)
        regroup(d)
        quantise(b)
        sigmoid(a - 1)
        turn_back(a - 2, bankp, "back")
        quantise(d)
        stage2(a, bank1, "acc1")
        stage2(b, bank1, "acc1")
        stage2(d, bank1, "acc1")
        mix(a - 2)
        turn_back(a - 1, bank2, "acc2")
        mix(a - 1)
        sigmoid(a)
        sigmoid(b)
        sigmoid(d)
        turn_back(a, bankp, "back")
        mix(a)
        turn_back(b, bankx, "turned")
        mix(b)
        turn_back(d, bankx, "turned")
        mix(d)
